import numpy as np
import ml_dtypes


def mxq(x, axis, fmt="e4m3"):
    dtype, down = {"e4m3": (ml_dtypes.float8_e4m3fn, 7), "e5m2": (ml_dtypes.float8_e5m2, 14)}[fmt]
    v = np.moveaxis(np.asarray(x, np.float32).astype(ml_dtypes.bfloat16).astype(np.float64), axis, -1)
    blocks = v.reshape(v.shape[:-1] + (-1, 32))
    amax = np.abs(blocks).max(-1, keepdims=True)
    byte = np.maximum(np.where(amax > 0, np.frexp(amax)[1] - 1 + 127, 0) - down, 1)
    scale = np.exp2(byte - 127.0)
    codes = (blocks / scale).astype(np.float32).astype(dtype).astype(np.float64)
    return np.moveaxis((codes * scale).reshape(v.shape), -1, axis)


WIDE = False


def mx_kscale(k):
    if not WIDE:
        return np.ones(k)
    levels = np.array([10, -10, 5, -5, 0])
    if k % 512:
        return np.exp2(np.random.permutation(np.resize(levels, k // 32))).repeat(32)
    a = np.empty((k // 512, 16))
    for p in range(k // 512):
        a[p, :8] = np.random.permutation(np.resize(levels, 8))
        for g in range(8):
            far = levels[np.abs(levels - a[p, g]) >= 10]
            a[p, g + 8] = far[np.random.randint(len(far))]
    return np.exp2(a.ravel()).repeat(32)


BF16 = ml_dtypes.bfloat16


def bf(x):
    return np.asarray(x, np.float32).astype(BF16)


def f64(x):
    return np.asarray(x).astype(np.float64)


B, L, D, H, P, W = 2, 192, 1024, 4, 128, 128
HD = D // H
LT = L + P


def rotate_half(t):
    h = t.shape[-1] // 2
    return np.concatenate([-t[..., h:], t[..., :h]], axis=-1)


def project(pq, xq, w):
    wm = mxq(f64(w), 0, "e4m3")
    tp = pq @ wm
    tx = xq @ wm
    return np.concatenate([np.broadcast_to(tp, (B, P, D)), tx], axis=1).reshape(B, LT, H, HD)


def draw0():
    s = mx_kscale(D)
    return {"x": bf(np.random.standard_normal((B, L, D)) * s),
            "pmem": bf(np.random.standard_normal((1, P, D)) * s),
            "cos": bf(np.random.uniform(size=(LT, HD))),
            "sin": bf(np.random.uniform(size=(LT, HD))),
            "wq": bf(np.random.standard_normal((D, D)) / np.sqrt(D) / s[:, None]),
            "wk": bf(np.random.standard_normal((D, D)) / np.sqrt(D) / s[:, None]),
            "wv": bf(np.random.standard_normal((D, D)) / np.sqrt(D) / s[:, None])}


def core(x, pmem, cos, sin, wq, wk, wv):
    pq = mxq(f64(pmem), 2, "e4m3")
    xq = mxq(f64(x), 2, "e4m3")
    q = project(pq, xq, wq)
    k = project(pq, xq, wk)
    v = project(pq, xq, wv)
    cc = f64(cos)[None, :, None, :]
    ss = f64(sin)[None, :, None, :]
    q = q * cc + rotate_half(q) * ss
    k = k * cc + rotate_half(k) * ss
    return q, k, v


def e4m3fn_bytes(y):
    return np.clip(np.asarray(y, np.float64), -448.0, 448.0).astype(np.float32).astype(ml_dtypes.float8_e4m3fn).view(np.uint8)


def e4m3fn_values(b):
    return np.asarray(b, np.uint8).view(ml_dtypes.float8_e4m3fn).astype(np.float64)


def setup_inputs():
    d = draw0()
    x0 = np.asarray(d['wv']).astype(np.float64)
    s = (np.max(np.abs(x0), axis=(1,), keepdims=True) / 448.0).astype(np.float32)
    out = {}
    for k, v in d.items():
        if k == 'wv':
            out['wv_bytes'] = e4m3fn_bytes(x0 / s.astype(np.float64))
            out['wv_scale'] = s
        else:
            out[k] = v
    return out


def reference(x, pmem, cos, sin, wq, wk, wv_bytes, wv_scale):
    return core(x, pmem, cos, sin, wq, wk, e4m3fn_values(wv_bytes) * wv_scale.astype(np.float64))

@@ -1,0 +1,287 @@
+from contextlib import ExitStack
+
+import concourse.mybir as mybir
+from concourse.masks import make_identity
+
+FLOPS = 2 * 640 * 1024 * 3072
+
+F32 = mybir.dt.float32
+BF16 = mybir.dt.bfloat16
+U32 = mybir.dt.uint32
+U8 = mybir.dt.uint8
+FP8 = mybir.dt.float8_e4m3fn
+FP8X4 = mybir.dt.float8_e4m3fn_x4
+ALU = mybir.AluOpType
+ACT = mybir.ActivationFunctionType
+
+P = 128
+PACK = 4
+D = 1024
+NH = 512
+HEAD = 256
+HALF = 128
+X_REST = 64
+WQ, WK, WV = 0, 1, 2
+
+TABLE_OF_TILE = (0, 1, 1, 2)
+TILE_ORDER = (3, 0, 1, 2)
+
+ITEM_BANKS = 4
+V_BANKS = 4
+ROT_BUFS = 4
+V_OUT_BUFS = 8
+
+
+def tile_titanstnt_pa_kernel(tc, x, pmem, cos, sin, wq, wk, wv_bytes, wv_scale, out_0, out_1, out_2):
+    nc = tc.nc
+    with ExitStack() as ctx:
+        keep = ctx.enter_context(tc.tile_pool(name="keep", bufs=1))
+        work = ctx.enter_context(tc.tile_pool(name="work", bufs=ROT_BUFS))
+        item_psum = ctx.enter_context(tc.psum_pool(name="item_psum", bufs=ITEM_BANKS))
+        v_psum = ctx.enter_context(tc.psum_pool(name="v_psum", bufs=V_BANKS))
+        ctx.enter_context(tc.manual_schedule())
+
+        outs = [o.rearrange("b t h d -> b t (h d)") for o in (out_0, out_1, out_2)]
+
+        warm_in = keep.tile([P, 8], F32, name="warm_in", tag="warm_in")
+        warm_out = keep.tile([P, 8], F32, name="warm_out", tag="warm_out")
+        nc.vector.memset(warm_in[:], 0.0)
+        nc.scalar.activation(out=warm_out[:], in_=warm_in[:], func=ACT.Copy)
+        ident = keep.tile([P, P], F32, name="ident", tag="ident")
+        make_identity(nc, ident[:])
+
+        wq_view = wq.rearrange("(g p j) n -> g p j n", p=P, j=PACK)
+        wk_view = wk.rearrange("(g p j) n -> g p j n", p=P, j=PACK)
+        wv_view = wv_bytes.rearrange("(g p j) n -> g p j n", p=P, j=PACK)
+        rows = {}
+
+        def load_wq_unit(g, nh):
+            t = keep.tile([P, PACK, NH], BF16, name="wq_rows%d%d" % (g, nh), tag="wq_rows%d%d" % (g, nh))
+            nc.sync.dma_start(out=t[:], in_=wq_view[g][:, :, nh * NH:(nh + 1) * NH])
+            rows[(WQ, g, nh)] = t[:]
+
+        load_wq_unit(0, 0)
+        load_wq_unit(1, 0)
+        load_wq_unit(0, 1)
+        x_pmem = keep.tile([P, D], BF16, name="x_pmem", tag="x_pmem")
+        nc.sync.dma_start(out=x_pmem[:], in_=pmem[0])
+        x_first = keep.tile([P, 2, D], BF16, name="x_first", tag="x_first")
+        nc.sync.dma_start(out=x_first[:], in_=x[:, 0:P, :].rearrange("b p k -> p b k"))
+        x_rest = keep.tile([P, D], BF16, name="x_rest", tag="x_rest")
+        for b in range(2):
+            nc.sync.dma_start(out=x_rest[X_REST * b:X_REST * (b + 1), :], in_=x[b, P:P + X_REST, :])
+        load_wq_unit(1, 1)
+        wv_scales = keep.tile([P, 2, PACK], F32, name="wv_scales", tag="wv_scales")
+        nc.sync.dma_start(out=wv_scales[:], in_=wv_scale.rearrange("(g p j) o -> p g (j o)", p=P, j=PACK))
+        wv_codes_in = [keep.tile([P, PACK, D], U8, name="wv_codes_in%d" % g, tag="wv_codes_in%d" % g) for g in range(2)]
+        for g in range(2):
+            nc.sync.dma_start(out=wv_codes_in[g][:], in_=wv_view[g])
+        cos_tab = keep.tile([P, 3, HEAD], BF16, name="cos_tab", tag="cos_tab")
+        sin_tab = keep.tile([P, 3, HEAD], BF16, name="sin_tab", tag="sin_tab")
+        for tab, src in ((cos_tab, cos), (sin_tab, sin)):
+            nc.sync.dma_start(out=tab[:, 0:2, :], in_=src[0:2 * P, :].rearrange("(a p) d -> p a d", p=P))
+            for b in range(2):
+                nc.sync.dma_start(out=tab[X_REST * b:X_REST * (b + 1), 2, :], in_=src[2 * P:2 * P + X_REST, :])
+        for g in range(2):
+            t = keep.tile([P, PACK, D], BF16, name="wk_rows%d" % g, tag="wk_rows%d" % g)
+            nc.sync.dma_start(out=t[:], in_=wk_view[g])
+            for nh in range(2):
+                rows[(WK, g, nh)] = t[:, :, nh * NH:(nh + 1) * NH]
+
+        w_codes = [keep.tile([P, 4, NH], U32, name="w_codes%d" % w, tag="w_codes%d" % w, align_bytes=64) for w in range(3)]
+        w_scales = [keep.tile([P, 4, NH], U8, name="w_scales%d" % w, tag="w_scales%d" % w, align_bytes=64) for w in range(3)]
+        x_grouped = keep.tile([P, 2, 4 * P, PACK], BF16, name="x_grouped", tag="x_grouped", align_bytes=64)
+        x_codes = keep.tile([P, 2, 4 * P], U32, name="x_codes", tag="x_codes", align_bytes=64)
+        x_scales = keep.tile([P, 2, 4 * P], U8, name="x_scales", tag="x_scales", align_bytes=64)
+        grouped = {}
+
+        def place(w, g, nh):
+            return 2 * g + nh if w == WK else 2 * nh + g
+
+        def interleave(copy, w, g, nh):
+            at = place(w, g, nh)
+            if (w, at // 2) not in grouped:
+                tag = "grouped%d%d" % (w % 2, at // 2)
+                grouped[(w, at // 2)] = keep.tile([P, 2, NH, PACK], BF16, name=tag, tag=tag, align_bytes=64)
+            copy(out=grouped[(w, at // 2)][:, at % 2, :, :], in_=rows[(w, g, nh)].rearrange("p j c -> p c j"))
+
+        def quantize_unit(w, g, nh):
+            at = place(w, g, nh)
+            nc.vector.quantize_mx(
+                out=w_codes[w][:, at, :].bitcast(FP8X4),
+                scales=w_scales[w][:, at, :],
+                in_=grouped[(w, at // 2)][:, at % 2, :, :].rearrange("p c j -> p (c j)"),
+            )
+
+        def quantize_pair(w, pair):
+            nc.vector.quantize_mx(
+                out=w_codes[w][:, 2 * pair:2 * pair + 2, :].rearrange("p s c -> p (s c)").bitcast(FP8X4),
+                scales=w_scales[w][:, 2 * pair:2 * pair + 2, :].rearrange("p s c -> p (s c)"),
+                in_=grouped[(w, pair)][:].rearrange("p s c j -> p (s c j)"),
+            )
+
+        wv_rows = [keep.tile([P, PACK, D], BF16, name="wv_rows%d" % g, tag="wv_rows%d" % g) for g in range(2)]
+        for g in range(2):
+            for nh in range(2):
+                rows[(WV, g, nh)] = wv_rows[g][:, :, nh * NH:(nh + 1) * NH]
+
+        def widen_on_scalar(g):
+            for j in range(PACK):
+                nc.scalar.activation(
+                    out=wv_rows[g][:, j, :], in_=wv_codes_in[g][:, j, :].bitcast(FP8), func=ACT.Copy, scale=wv_scales[:, g, j:j + 1]
+                )
+
+        def widen_on_vector(g):
+            for j in range(PACK):
+                nc.vector.tensor_scalar(
+                    out=wv_rows[g][:, j, :], in0=wv_codes_in[g][:, j, :].bitcast(FP8), scalar1=wv_scales[:, g, j:j + 1], scalar2=None, op0=ALU.mult
+                )
+
+        interleave(nc.vector.tensor_copy, WQ, 0, 0)
+        interleave(nc.scalar.copy, WQ, 1, 0)
+        interleave(nc.vector.tensor_copy, WQ, 0, 1)
+        quantize_unit(WQ, 0, 0)
+        quantize_unit(WQ, 0, 1)
+        quantize_unit(WQ, 1, 0)
+        interleave(nc.vector.tensor_copy, WQ, 1, 1)
+
+        x_words = [x_pmem[:].bitcast(F32), x_first[:, 0, :].bitcast(F32), x_first[:, 1, :].bitcast(F32), x_rest[:].bitcast(F32)]
+        words_of_pass = NH // 2
+        for g in range(2):
+            for tile_pair in range(2):
+                turned = item_psum.tile([P, 2, 2, P], F32, name="turned", tag="bank")
+                for i in range(2):
+                    for u in range(2):
+                        nc.tensor.transpose(
+                            turned[:, i, u, :], x_words[2 * tile_pair + i][:, words_of_pass * g + u:words_of_pass * (g + 1):2], ident[:]
+                        )
+                dst = x_grouped[:, g, 2 * P * tile_pair:2 * P * (tile_pair + 1), :].rearrange("p r t -> p (r t)").bitcast(F32)
+                nc.scalar.copy(out=dst.rearrange("p (i r u) -> p i r u", i=2, u=2), in_=turned[:].rearrange("p i u r -> p i r u"))
+        for g in range(2):
+            nc.vector.quantize_mx(
+                out=x_codes[:, g, :].bitcast(FP8X4),
+                scales=x_scales[:, g, :],
+                in_=x_grouped[:, g, :, :].rearrange("p r t -> p (r t)"),
+            )
+        quantize_unit(WQ, 1, 1)
+        sin_swapped = keep.tile([P, 3, HEAD], BF16, name="sin_swapped", tag="sin_swapped")
+        nc.vector.tensor_copy(out=sin_swapped[:, :, 0:HALF], in_=sin_tab[:, :, HALF:HEAD])
+        nc.vector.tensor_copy(out=sin_swapped[:, :, HALF:HEAD], in_=sin_tab[:, :, 0:HALF])
+        widen_on_scalar(0)
+        for g in range(2):
+            for nh in range(2):
+                interleave(nc.scalar.copy, WK, g, nh)
+        widen_on_vector(1)
+
+        def multiply(pool, w, m, nh):
+            bank = pool.tile([P, NH], F32, name="bank", tag="bank")
+            for g in range(2):
+                at = place(w, g, nh)
+                nc.tensor.matmul_mx(
+                    out=bank[:],
+                    lhsT=x_codes[:, g, m * P:(m + 1) * P].bitcast(FP8X4),
+                    lhsT_scale=x_scales[:, g, m * P:(m + 1) * P],
+                    rhs=w_codes[w][:, at, :].bitcast(FP8X4),
+                    rhs_scale=w_scales[w][:, at, :],
+                    start=(g == 0),
+                    stop=(g == 1),
+                )
+            return bank
+
+        def store(w, m, src, cols):
+            out = outs[w]
+            if m == 0:
+                for b in range(2):
+                    nc.sync.dma_start(out=out[b, 0:P, cols], in_=src)
+            elif m < 3:
+                nc.sync.dma_start(out=out[m - 1, P:2 * P, cols], in_=src)
+            else:
+                for b in range(2):
+                    nc.sync.dma_start(out=out[b, 2 * P:2 * P + X_REST, cols], in_=src[X_REST * b:X_REST * (b + 1), :])
+
+        items = [(w, m) for w in (WQ, WK) for m in TILE_ORDER]
+        item_banks = {}
+        by_cos = {}
+        by_sin = {}
+        rotated = {}
+
+        def matmuls(i):
+            w, m = items[i]
+            item_banks[i] = [multiply(item_psum, w, m, nh) for nh in range(2)]
+
+        def products(i, nh):
+            m = items[i][1]
+            if nh == 0:
+                by_cos[i] = work.tile([P, D], F32, name="by_cos", tag="by_cos")
+                by_sin[i] = work.tile([P, D], F32, name="by_sin", tag="by_sin")
+            sums = item_banks[i][nh][:].rearrange("p (h d) -> p h d", d=HEAD)
+            for dst, tab in ((by_cos[i], cos_tab), (by_sin[i], sin_swapped)):
+                nc.vector.tensor_tensor(
+                    out=dst[:, nh * NH:(nh + 1) * NH].rearrange("p (h d) -> p h d", d=HEAD),
+                    in0=sums,
+                    in1=tab[:, TABLE_OF_TILE[m], :].unsqueeze(1).to_broadcast([P, NH // HEAD, HEAD]),
+                    op=ALU.mult,
+                )
+
+        def cross_add(engine, i, h0, h1):
+            w, m = items[i]
+            if h0 == 0:
+                rotated[i] = work.tile([P, D], F32, name="rotated", tag="rotated")
+            r = rotated[i][:].rearrange("p (h u f) -> p h u f", u=2, f=HALF)
+            c = by_cos[i][:].rearrange("p (h u f) -> p h u f", u=2, f=HALF)
+            s = by_sin[i][:].rearrange("p (h u f) -> p h u f", u=2, f=HALF)
+            engine.tensor_tensor(out=r[:, h0:h1, 0, :], in0=c[:, h0:h1, 0, :], in1=s[:, h0:h1, 1, :], op=ALU.subtract)
+            engine.tensor_tensor(out=r[:, h0:h1, 1, :], in0=c[:, h0:h1, 1, :], in1=s[:, h0:h1, 0, :], op=ALU.add)
+            cols = slice(h0 * HEAD, h1 * HEAD)
+            store(w, m, rotated[i][:, cols], cols)
+
+        def rotate(i):
+            products(i, 0)
+            products(i, 1)
+            cross_add(nc.gpsimd, i, 0, 4)
+
+        v_banks = {}
+
+        def matmuls_v(nh):
+            for m in TILE_ORDER:
+                v_banks[(nh, m)] = multiply(v_psum, WV, m, nh)
+
+        def copy_out_v(nh):
+            for m in TILE_ORDER:
+                v_out = work.tile([P, NH], F32, name="v_out", tag="v_out", bufs=V_OUT_BUFS)
+                nc.scalar.copy(out=v_out[:], in_=v_banks[(nh, m)][:])
+                store(WV, m, v_out[:], slice(nh * NH, (nh + 1) * NH))
+
+        matmuls(0)
+        matmuls(1)
+        rotate(0)
+        matmuls(2)
+        rotate(1)
+        matmuls(3)
+        rotate(2)
+        quantize_pair(WK, 0)
+        products(3, 0)
+        quantize_pair(WK, 1)
+        matmuls(4)
+        products(3, 1)
+        cross_add(nc.gpsimd, 3, 0, 4)
+        matmuls(5)
+        interleave(nc.scalar.copy, WV, 0, 0)
+        interleave(nc.scalar.copy, WV, 1, 0)
+        rotate(4)
+        matmuls(6)
+        quantize_pair(WV, 0)
+        matmuls_v(0)
+        interleave(nc.scalar.copy, WV, 0, 1)
+        interleave(nc.scalar.copy, WV, 1, 1)
+        copy_out_v(0)
+        rotate(5)
+        matmuls(7)
+        quantize_pair(WV, 1)
+        matmuls_v(1)
+        copy_out_v(1)
+        rotate(6)
+        products(7, 0)
+        cross_add(nc.gpsimd, 7, 0, 2)
+        products(7, 1)
+        cross_add(nc.vector, 7, 2, 4)

@@ -69,7 +69,7 @@ def tile_titanstnt_pa_kernel(tc, x, pmem, cos, sin, wq, wk, wv_bytes, wv_scale, 
         nc.sync.dma_start(out=x_first[:], in_=x[:, 0:P, :].rearrange("b p k -> p b k"))
         x_rest = keep.tile([P, D], BF16, name="x_rest", tag="x_rest")
         for b in range(2):
-            nc.sync.dma_start(out=x_rest[X_REST * b:X_REST * (b + 1), :], in_=x[b, P:P + X_REST, :])
+            nc.sync.dma_start(out=x_rest[b:P:2, :], in_=x[b, P:P + X_REST, :])
         load_wq_unit(1, 1)
         wv_scales = keep.tile([P, 2, PACK], F32, name="wv_scales", tag="wv_scales")
         nc.sync.dma_start(out=wv_scales[:], in_=wv_scale.rearrange("(g p j) o -> p g (j o)", p=P, j=PACK))
@@ -81,7 +81,7 @@ def tile_titanstnt_pa_kernel(tc, x, pmem, cos, sin, wq, wk, wv_bytes, wv_scale, 
         for tab, src in ((cos_tab, cos), (sin_tab, sin)):
             nc.sync.dma_start(out=tab[:, 0:2, :], in_=src[0:2 * P, :].rearrange("(a p) d -> p a d", p=P))
             for b in range(2):
-                nc.sync.dma_start(out=tab[X_REST * b:X_REST * (b + 1), 2, :], in_=src[2 * P:2 * P + X_REST, :])
+                nc.sync.dma_start(out=tab[b:P:2, 2, :], in_=src[2 * P:2 * P + X_REST, :])
         for g in range(2):
             t = keep.tile([P, PACK, D], BF16, name="wk_rows%d" % g, tag="wk_rows%d" % g)
             nc.sync.dma_start(out=t[:], in_=wk_view[g])
@@ -197,7 +197,7 @@ def tile_titanstnt_pa_kernel(tc, x, pmem, cos, sin, wq, wk, wv_bytes, wv_scale, 
                 nc.sync.dma_start(out=out[m - 1, P:2 * P, cols], in_=src)
             else:
                 for b in range(2):
-                    nc.sync.dma_start(out=out[b, 2 * P:2 * P + X_REST, cols], in_=src[X_REST * b:X_REST * (b + 1), :])
+                    nc.sync.dma_start(out=out[b, 2 * P:2 * P + X_REST, cols], in_=src[b:P:2, :])
 
         items = [(w, m) for w in (WQ, WK) for m in TILE_ORDER]
         item_banks = {}

@@ -21,6 +21,7 @@ NH = 512
 HEAD = 256
 HALF = 128
 X_REST = 64
+RUN = 4
 WQ, WK, WV = 0, 1, 2
 
 TABLE_OF_TILE = (0, 1, 1, 2)
@@ -103,7 +104,10 @@ def tile_titanstnt_pa_kernel(tc, x, pmem, cos, sin, wq, wk, wv_bytes, wv_scale, 
             if (w, at // 2) not in grouped:
                 tag = "grouped%d%d" % (w % 2, at // 2)
                 grouped[(w, at // 2)] = keep.tile([P, 2, NH, PACK], BF16, name=tag, tag=tag, align_bytes=64)
-            copy(out=grouped[(w, at // 2)][:, at % 2, :, :], in_=rows[(w, g, nh)].rearrange("p j c -> p c j"))
+            copy(
+                out=grouped[(w, at // 2)][:, at % 2, :, :].rearrange("p (c i) j -> p c j i", i=RUN),
+                in_=rows[(w, g, nh)].rearrange("p j (c i) -> p c j i", i=RUN),
+            )
 
         def quantize_unit(w, g, nh):
             at = place(w, g, nh)

@@ -61,6 +61,10 @@ def tile_titanstnt_pa_kernel(tc, x, pmem, cos, sin, wq, wk, wv_bytes, wv_scale, 
             nc.sync.dma_start(out=t[:], in_=wq_view[g][:, :, nh * NH:(nh + 1) * NH])
             rows[(WQ, g, nh)] = t[:]
 
+        wv_scales = keep.tile([P, 2, PACK], F32, name="wv_scales", tag="wv_scales")
+        nc.sync.dma_start(out=wv_scales[:], in_=wv_scale.rearrange("(g p j) o -> p g (j o)", p=P, j=PACK))
+        wv_codes_in = [keep.tile([P, PACK, D], U8, name="wv_codes_in%d" % g, tag="wv_codes_in%d" % g) for g in range(2)]
+        nc.sync.dma_start(out=wv_codes_in[0][:], in_=wv_view[0])
         load_wq_unit(0, 0)
         load_wq_unit(1, 0)
         load_wq_unit(0, 1)
@@ -72,11 +76,7 @@ def tile_titanstnt_pa_kernel(tc, x, pmem, cos, sin, wq, wk, wv_bytes, wv_scale, 
         for b in range(2):
             nc.sync.dma_start(out=x_rest[b:P:2, :], in_=x[b, P:P + X_REST, :])
         load_wq_unit(1, 1)
-        wv_scales = keep.tile([P, 2, PACK], F32, name="wv_scales", tag="wv_scales")
-        nc.sync.dma_start(out=wv_scales[:], in_=wv_scale.rearrange("(g p j) o -> p g (j o)", p=P, j=PACK))
-        wv_codes_in = [keep.tile([P, PACK, D], U8, name="wv_codes_in%d" % g, tag="wv_codes_in%d" % g) for g in range(2)]
-        for g in range(2):
-            nc.sync.dma_start(out=wv_codes_in[g][:], in_=wv_view[g])
+        nc.sync.dma_start(out=wv_codes_in[1][:], in_=wv_view[1])
         cos_tab = keep.tile([P, 3, HEAD], BF16, name="cos_tab", tag="cos_tab")
         sin_tab = keep.tile([P, 3, HEAD], BF16, name="sin_tab", tag="sin_tab")
         for tab, src in ((cos_tab, cos), (sin_tab, sin)):
@@ -97,12 +97,12 @@ def tile_titanstnt_pa_kernel(tc, x, pmem, cos, sin, wq, wk, wv_bytes, wv_scale, 
         grouped = {}
 
         def place(w, g, nh):
-            return 2 * g + nh if w == WK else 2 * nh + g
+            return 2 * nh + g
 
         def interleave(copy, w, g, nh):
             at = place(w, g, nh)
             if (w, at // 2) not in grouped:
-                tag = "grouped%d%d" % (w % 2, at // 2)
+                tag = "grouped%d%d" % (w // 2, at // 2)
                 grouped[(w, at // 2)] = keep.tile([P, 2, NH, PACK], BF16, name=tag, tag=tag, align_bytes=64)
             copy(
                 out=grouped[(w, at // 2)][:, at % 2, :, :].rearrange("p (c i) j -> p c j i", i=RUN),
@@ -141,13 +141,14 @@ def tile_titanstnt_pa_kernel(tc, x, pmem, cos, sin, wq, wk, wv_bytes, wv_scale, 
                     out=wv_rows[g][:, j, :], in0=wv_codes_in[g][:, j, :].bitcast(FP8), scalar1=wv_scales[:, g, j:j + 1], scalar2=None, op0=ALU.mult
                 )
 
+        widen_on_scalar(0)
         interleave(nc.vector.tensor_copy, WQ, 0, 0)
-        interleave(nc.scalar.copy, WQ, 1, 0)
+        interleave(nc.vector.tensor_copy, WQ, 1, 0)
         interleave(nc.vector.tensor_copy, WQ, 0, 1)
         quantize_unit(WQ, 0, 0)
-        quantize_unit(WQ, 0, 1)
         quantize_unit(WQ, 1, 0)
-        interleave(nc.vector.tensor_copy, WQ, 1, 1)
+        quantize_unit(WQ, 0, 1)
+        interleave(nc.scalar.copy, WV, 0, 0)
 
         x_words = [x_pmem[:].bitcast(F32), x_first[:, 0, :].bitcast(F32), x_first[:, 1, :].bitcast(F32), x_rest[:].bitcast(F32)]
         words_of_pass = NH // 2
@@ -161,6 +162,11 @@ def tile_titanstnt_pa_kernel(tc, x, pmem, cos, sin, wq, wk, wv_bytes, wv_scale, 
                         )
                 dst = x_grouped[:, g, 2 * P * tile_pair:2 * P * (tile_pair + 1), :].rearrange("p r t -> p (r t)").bitcast(F32)
                 nc.scalar.copy(out=dst.rearrange("p (i r u) -> p i r u", i=2, u=2), in_=turned[:].rearrange("p i u r -> p i r u"))
+        interleave(nc.vector.tensor_copy, WQ, 1, 1)
+        widen_on_vector(1)
+        sin_swapped = keep.tile([P, 3, HEAD], BF16, name="sin_swapped", tag="sin_swapped")
+        nc.vector.tensor_copy(out=sin_swapped[:, :, 0:HALF], in_=sin_tab[:, :, HALF:HEAD])
+        nc.vector.tensor_copy(out=sin_swapped[:, :, HALF:HEAD], in_=sin_tab[:, :, 0:HALF])
         for g in range(2):
             nc.vector.quantize_mx(
                 out=x_codes[:, g, :].bitcast(FP8X4),
@@ -168,14 +174,12 @@ def tile_titanstnt_pa_kernel(tc, x, pmem, cos, sin, wq, wk, wv_bytes, wv_scale, 
                 in_=x_grouped[:, g, :, :].rearrange("p r t -> p (r t)"),
             )
         quantize_unit(WQ, 1, 1)
-        sin_swapped = keep.tile([P, 3, HEAD], BF16, name="sin_swapped", tag="sin_swapped")
-        nc.vector.tensor_copy(out=sin_swapped[:, :, 0:HALF], in_=sin_tab[:, :, HALF:HEAD])
-        nc.vector.tensor_copy(out=sin_swapped[:, :, HALF:HEAD], in_=sin_tab[:, :, 0:HALF])
-        widen_on_scalar(0)
-        for g in range(2):
-            for nh in range(2):
+        interleave(nc.scalar.copy, WV, 0, 1)
+        for nh in range(2):
+            for g in range(2):
                 interleave(nc.scalar.copy, WK, g, nh)
-        widen_on_vector(1)
+        for nh in range(2):
+            interleave(nc.scalar.copy, WV, 1, nh)
 
         def multiply(pool, w, m, nh):
             bank = pool.tile([P, NH], F32, name="bank", tag="bank")
@@ -268,22 +272,18 @@ def tile_titanstnt_pa_kernel(tc, x, pmem, cos, sin, wq, wk, wv_bytes, wv_scale, 
         quantize_pair(WK, 1)
         matmuls(4)
         products(3, 1)
-        cross_add(nc.gpsimd, 3, 0, 4)
-        matmuls(5)
-        interleave(nc.scalar.copy, WV, 0, 0)
-        interleave(nc.scalar.copy, WV, 1, 0)
-        rotate(4)
-        matmuls(6)
         quantize_pair(WV, 0)
         matmuls_v(0)
-        interleave(nc.scalar.copy, WV, 0, 1)
-        interleave(nc.scalar.copy, WV, 1, 1)
+        matmuls(5)
         copy_out_v(0)
-        rotate(5)
-        matmuls(7)
+        cross_add(nc.gpsimd, 3, 0, 4)
+        rotate(4)
+        matmuls(6)
         quantize_pair(WV, 1)
         matmuls_v(1)
         copy_out_v(1)
+        rotate(5)
+        matmuls(7)
         rotate(6)
         products(7, 0)
         cross_add(nc.gpsimd, 7, 0, 2)

@@ -199,8 +199,8 @@ def tile_titanstnt_pa_kernel(tc, x, pmem, cos, sin, wq, wk, wv_bytes, wv_scale, 
         def store(w, m, src, cols):
             out = outs[w]
             if m == 0:
-                for b in range(2):
-                    nc.sync.dma_start(out=out[b, 0:P, cols], in_=src)
+                width = src.shape[1]
+                nc.sync.dma_start(out=out[:, 0:P, cols].rearrange("b p c -> p b c"), in_=src.unsqueeze(1).to_broadcast([P, 2, width]))
             elif m < 3:
                 nc.sync.dma_start(out=out[m - 1, P:2 * P, cols], in_=src)
             else:

@@ -21,7 +21,7 @@ NH = 512
 HEAD = 256
 HALF = 128
 X_REST = 64
-RUN = 4
+RUN = 8
 WQ, WK, WV = 0, 1, 2
 
 TABLE_OF_TILE = (0, 1, 1, 2)

@@ -30,7 +30,7 @@ TILE_ORDER = (3, 0, 1, 2)
 ITEM_BANKS = 4
 V_BANKS = 4
 ROT_BUFS = 4
-V_OUT_BUFS = 8
+V_OUT_BUFS = 4
 
 
 def tile_titanstnt_pa_kernel(tc, x, pmem, cos, sin, wq, wk, wv_bytes, wv_scale, out_0, out_1, out_2):
@@ -164,9 +164,6 @@ def tile_titanstnt_pa_kernel(tc, x, pmem, cos, sin, wq, wk, wv_bytes, wv_scale, 
                 nc.scalar.copy(out=dst.rearrange("p (i r u) -> p i r u", i=2, u=2), in_=turned[:].rearrange("p i u r -> p i r u"))
         interleave(nc.vector.tensor_copy, WQ, 1, 1)
         widen_on_vector(1)
-        sin_swapped = keep.tile([P, 3, HEAD], BF16, name="sin_swapped", tag="sin_swapped")
-        nc.vector.tensor_copy(out=sin_swapped[:, :, 0:HALF], in_=sin_tab[:, :, HALF:HEAD])
-        nc.vector.tensor_copy(out=sin_swapped[:, :, HALF:HEAD], in_=sin_tab[:, :, 0:HALF])
         for g in range(2):
             nc.vector.quantize_mx(
                 out=x_codes[:, g, :].bitcast(FP8X4),
@@ -175,6 +172,9 @@ def tile_titanstnt_pa_kernel(tc, x, pmem, cos, sin, wq, wk, wv_bytes, wv_scale, 
             )
         quantize_unit(WQ, 1, 1)
         interleave(nc.scalar.copy, WV, 0, 1)
+        sin_swapped = keep.tile([P, 3, HEAD], BF16, name="sin_swapped", tag="sin_swapped")
+        nc.scalar.copy(out=sin_swapped[:, :, 0:HALF], in_=sin_tab[:, :, HALF:HEAD])
+        nc.scalar.copy(out=sin_swapped[:, :, HALF:HEAD], in_=sin_tab[:, :, 0:HALF])
         for nh in range(2):
             for g in range(2):
                 interleave(nc.scalar.copy, WK, g, nh)
@@ -255,10 +255,15 @@ def tile_titanstnt_pa_kernel(tc, x, pmem, cos, sin, wq, wk, wv_bytes, wv_scale, 
                 v_banks[(nh, m)] = multiply(v_psum, WV, m, nh)
 
         def copy_out_v(nh):
-            for m in TILE_ORDER:
+            cols = slice(nh * NH, (nh + 1) * NH)
+            for m in (3, 0):
                 v_out = work.tile([P, NH], F32, name="v_out", tag="v_out", bufs=V_OUT_BUFS)
                 nc.scalar.copy(out=v_out[:], in_=v_banks[(nh, m)][:])
-                store(WV, m, v_out[:], slice(nh * NH, (nh + 1) * NH))
+                store(WV, m, v_out[:], cols)
+            v_both = work.tile([P, 2, NH], F32, name="v_both", tag="v_both", bufs=2)
+            for b in range(2):
+                nc.scalar.copy(out=v_both[:, b, :], in_=v_banks[(nh, 1 + b)][:])
+            nc.sync.dma_start(out=outs[WV][:, P:2 * P, cols].rearrange("b p c -> p b c"), in_=v_both[:])
 
         matmuls(0)
         matmuls(1)

@@ -172,9 +172,7 @@ def tile_titanstnt_pa_kernel(tc, x, pmem, cos, sin, wq, wk, wv_bytes, wv_scale, 
             )
         quantize_unit(WQ, 1, 1)
         interleave(nc.scalar.copy, WV, 0, 1)
-        sin_swapped = keep.tile([P, 3, HEAD], BF16, name="sin_swapped", tag="sin_swapped")
-        nc.scalar.copy(out=sin_swapped[:, :, 0:HALF], in_=sin_tab[:, :, HALF:HEAD])
-        nc.scalar.copy(out=sin_swapped[:, :, HALF:HEAD], in_=sin_tab[:, :, 0:HALF])
+        nc.scalar.activation(out=sin_tab[:, :, 0:HALF], in_=sin_tab[:, :, 0:HALF], func=ACT.Copy, scale=-1.0)
         for nh in range(2):
             for g in range(2):
                 interleave(nc.scalar.copy, WK, g, nh)
@@ -222,31 +220,35 @@ def tile_titanstnt_pa_kernel(tc, x, pmem, cos, sin, wq, wk, wv_bytes, wv_scale, 
             if nh == 0:
                 by_cos[i] = work.tile([P, D], F32, name="by_cos", tag="by_cos")
                 by_sin[i] = work.tile([P, D], F32, name="by_sin", tag="by_sin")
-            sums = item_banks[i][nh][:].rearrange("p (h d) -> p h d", d=HEAD)
-            for dst, tab in ((by_cos[i], cos_tab), (by_sin[i], sin_swapped)):
-                nc.vector.tensor_tensor(
-                    out=dst[:, nh * NH:(nh + 1) * NH].rearrange("p (h d) -> p h d", d=HEAD),
-                    in0=sums,
-                    in1=tab[:, TABLE_OF_TILE[m], :].unsqueeze(1).to_broadcast([P, NH // HEAD, HEAD]),
-                    op=ALU.mult,
-                )
+            heads = NH // HEAD
+            nc.vector.tensor_tensor(
+                out=by_cos[i][:, nh * NH:(nh + 1) * NH].rearrange("p (h d) -> p h d", d=HEAD),
+                in0=item_banks[i][nh][:].rearrange("p (h d) -> p h d", d=HEAD),
+                in1=cos_tab[:, TABLE_OF_TILE[m], :].unsqueeze(1).to_broadcast([P, heads, HEAD]),
+                op=ALU.mult,
+            )
+            nc.vector.tensor_tensor(
+                out=by_sin[i][:, nh * NH:(nh + 1) * NH].rearrange("p (h u f) -> p h u f", u=2, f=HALF),
+                in0=item_banks[i][nh][:].rearrange("p (h u f) -> p h u f", u=2, f=HALF)[:, :, ::-1, :],
+                in1=sin_tab[:, TABLE_OF_TILE[m], :].rearrange("p (u f) -> p u f", u=2).unsqueeze(1).to_broadcast([P, heads, 2, HALF]),
+                op=ALU.mult,
+            )
 
-        def cross_add(engine, i, h0, h1):
-            w, m = items[i]
-            if h0 == 0:
+        def add_half(engine, i, nh):
+            if nh == 0:
                 rotated[i] = work.tile([P, D], F32, name="rotated", tag="rotated")
-            r = rotated[i][:].rearrange("p (h u f) -> p h u f", u=2, f=HALF)
-            c = by_cos[i][:].rearrange("p (h u f) -> p h u f", u=2, f=HALF)
-            s = by_sin[i][:].rearrange("p (h u f) -> p h u f", u=2, f=HALF)
-            engine.tensor_tensor(out=r[:, h0:h1, 0, :], in0=c[:, h0:h1, 0, :], in1=s[:, h0:h1, 1, :], op=ALU.subtract)
-            engine.tensor_tensor(out=r[:, h0:h1, 1, :], in0=c[:, h0:h1, 1, :], in1=s[:, h0:h1, 0, :], op=ALU.add)
-            cols = slice(h0 * HEAD, h1 * HEAD)
-            store(w, m, rotated[i][:, cols], cols)
+            cols = slice(nh * NH, (nh + 1) * NH)
+            engine.tensor_tensor(out=rotated[i][:, cols], in0=by_cos[i][:, cols], in1=by_sin[i][:, cols], op=ALU.add)
+
+        def store_item(i):
+            w, m = items[i]
+            store(w, m, rotated[i][:], slice(0, D))
 
         def rotate(i):
-            products(i, 0)
-            products(i, 1)
-            cross_add(nc.gpsimd, i, 0, 4)
+            for nh in range(2):
+                products(i, nh)
+                add_half(nc.gpsimd, i, nh)
+            store_item(i)
 
         v_banks = {}
 
@@ -274,14 +276,16 @@ def tile_titanstnt_pa_kernel(tc, x, pmem, cos, sin, wq, wk, wv_bytes, wv_scale, 
         rotate(2)
         quantize_pair(WK, 0)
         products(3, 0)
+        add_half(nc.gpsimd, 3, 0)
         quantize_pair(WK, 1)
         matmuls(4)
         products(3, 1)
+        add_half(nc.gpsimd, 3, 1)
+        store_item(3)
         quantize_pair(WV, 0)
         matmuls_v(0)
         matmuls(5)
         copy_out_v(0)
-        cross_add(nc.gpsimd, 3, 0, 4)
         rotate(4)
         matmuls(6)
         quantize_pair(WV, 1)
@@ -291,6 +295,8 @@ def tile_titanstnt_pa_kernel(tc, x, pmem, cos, sin, wq, wk, wv_bytes, wv_scale, 
         matmuls(7)
         rotate(6)
         products(7, 0)
-        cross_add(nc.gpsimd, 7, 0, 2)
         products(7, 1)
-        cross_add(nc.vector, 7, 2, 4)
+        for nh in range(2):
+            add_half(nc.vector, 7, nh)
+            cols = slice(nh * NH, (nh + 1) * NH)
+            store(items[7][0], items[7][1], rotated[7][:, cols], cols)

@@ -30,6 +30,7 @@ TILE_ORDER = (3, 0, 1, 2)
 ITEM_BANKS = 4
 V_BANKS = 4
 ROT_BUFS = 4
+PRODUCT_BUFS = 8
 V_OUT_BUFS = 4
 
 
@@ -65,6 +66,7 @@ def tile_titanstnt_pa_kernel(tc, x, pmem, cos, sin, wq, wk, wv_bytes, wv_scale, 
         nc.sync.dma_start(out=wv_scales[:], in_=wv_scale.rearrange("(g p j) o -> p g (j o)", p=P, j=PACK))
         wv_codes_in = [keep.tile([P, PACK, D], U8, name="wv_codes_in%d" % g, tag="wv_codes_in%d" % g) for g in range(2)]
         nc.sync.dma_start(out=wv_codes_in[0][:], in_=wv_view[0])
+        nc.sync.dma_start(out=wv_codes_in[1][:], in_=wv_view[1])
         load_wq_unit(0, 0)
         load_wq_unit(1, 0)
         load_wq_unit(0, 1)
@@ -76,7 +78,6 @@ def tile_titanstnt_pa_kernel(tc, x, pmem, cos, sin, wq, wk, wv_bytes, wv_scale, 
         for b in range(2):
             nc.sync.dma_start(out=x_rest[b:P:2, :], in_=x[b, P:P + X_REST, :])
         load_wq_unit(1, 1)
-        nc.sync.dma_start(out=wv_codes_in[1][:], in_=wv_view[1])
         cos_tab = keep.tile([P, 3, HEAD], BF16, name="cos_tab", tag="cos_tab")
         sin_tab = keep.tile([P, 3, HEAD], BF16, name="sin_tab", tag="sin_tab")
         for tab, src in ((cos_tab, cos), (sin_tab, sin)):
@@ -129,19 +130,21 @@ def tile_titanstnt_pa_kernel(tc, x, pmem, cos, sin, wq, wk, wv_bytes, wv_scale, 
             for nh in range(2):
                 rows[(WV, g, nh)] = wv_rows[g][:, :, nh * NH:(nh + 1) * NH]
 
-        def widen_on_scalar(g):
-            for j in range(PACK):
+        def widen_on_scalar(g, slots):
+            for j in slots:
                 nc.scalar.activation(
                     out=wv_rows[g][:, j, :], in_=wv_codes_in[g][:, j, :].bitcast(FP8), func=ACT.Copy, scale=wv_scales[:, g, j:j + 1]
                 )
 
-        def widen_on_vector(g):
-            for j in range(PACK):
+        def widen_on_vector(g, slots):
+            for j in slots:
                 nc.vector.tensor_scalar(
                     out=wv_rows[g][:, j, :], in0=wv_codes_in[g][:, j, :].bitcast(FP8), scalar1=wv_scales[:, g, j:j + 1], scalar2=None, op0=ALU.mult
                 )
 
-        widen_on_scalar(0)
+        for g in range(2):
+            widen_on_vector(g, (0, 1))
+            widen_on_scalar(g, (2, 3))
         interleave(nc.vector.tensor_copy, WQ, 0, 0)
         interleave(nc.vector.tensor_copy, WQ, 1, 0)
         interleave(nc.vector.tensor_copy, WQ, 0, 1)
@@ -149,6 +152,7 @@ def tile_titanstnt_pa_kernel(tc, x, pmem, cos, sin, wq, wk, wv_bytes, wv_scale, 
         quantize_unit(WQ, 1, 0)
         quantize_unit(WQ, 0, 1)
         interleave(nc.scalar.copy, WV, 0, 0)
+        interleave(nc.scalar.copy, WV, 1, 0)
 
         x_words = [x_pmem[:].bitcast(F32), x_first[:, 0, :].bitcast(F32), x_first[:, 1, :].bitcast(F32), x_rest[:].bitcast(F32)]
         words_of_pass = NH // 2
@@ -163,7 +167,6 @@ def tile_titanstnt_pa_kernel(tc, x, pmem, cos, sin, wq, wk, wv_bytes, wv_scale, 
                 dst = x_grouped[:, g, 2 * P * tile_pair:2 * P * (tile_pair + 1), :].rearrange("p r t -> p (r t)").bitcast(F32)
                 nc.scalar.copy(out=dst.rearrange("p (i r u) -> p i r u", i=2, u=2), in_=turned[:].rearrange("p i u r -> p i r u"))
         interleave(nc.vector.tensor_copy, WQ, 1, 1)
-        widen_on_vector(1)
         for g in range(2):
             nc.vector.quantize_mx(
                 out=x_codes[:, g, :].bitcast(FP8X4),
@@ -171,13 +174,12 @@ def tile_titanstnt_pa_kernel(tc, x, pmem, cos, sin, wq, wk, wv_bytes, wv_scale, 
                 in_=x_grouped[:, g, :, :].rearrange("p r t -> p (r t)"),
             )
         quantize_unit(WQ, 1, 1)
-        interleave(nc.scalar.copy, WV, 0, 1)
+        quantize_pair(WV, 0)
         nc.scalar.activation(out=sin_tab[:, :, 0:HALF], in_=sin_tab[:, :, 0:HALF], func=ACT.Copy, scale=-1.0)
-        for nh in range(2):
-            for g in range(2):
-                interleave(nc.scalar.copy, WK, g, nh)
-        for nh in range(2):
-            interleave(nc.scalar.copy, WV, 1, nh)
+        for g in range(2):
+            interleave(nc.scalar.copy, WV, g, 1)
+        for g in range(2):
+            interleave(nc.scalar.copy, WK, g, 0)
 
         def multiply(pool, w, m, nh):
             bank = pool.tile([P, NH], F32, name="bank", tag="bank")
@@ -205,55 +207,55 @@ def tile_titanstnt_pa_kernel(tc, x, pmem, cos, sin, wq, wk, wv_bytes, wv_scale, 
                 for b in range(2):
                     nc.sync.dma_start(out=out[b, 2 * P:2 * P + X_REST, cols], in_=src[b:P:2, :])
 
-        items = [(w, m) for w in (WQ, WK) for m in TILE_ORDER]
-        item_banks = {}
+        banks = {}
         by_cos = {}
         by_sin = {}
-        rotated = {}
+        rotated_q = {}
 
-        def matmuls(i):
-            w, m = items[i]
-            item_banks[i] = [multiply(item_psum, w, m, nh) for nh in range(2)]
+        def matmuls(w, m, nh):
+            banks[(w, m, nh)] = multiply(item_psum, w, m, nh)
 
-        def products(i, nh):
-            m = items[i][1]
-            if nh == 0:
-                by_cos[i] = work.tile([P, D], F32, name="by_cos", tag="by_cos")
-                by_sin[i] = work.tile([P, D], F32, name="by_sin", tag="by_sin")
+        def products(w, m, nh):
+            key = (w, m, nh)
+            by_cos[key] = work.tile([P, NH], F32, name="by_cos", tag="by_cos", bufs=PRODUCT_BUFS)
+            by_sin[key] = work.tile([P, NH], F32, name="by_sin", tag="by_sin", bufs=PRODUCT_BUFS)
             heads = NH // HEAD
             nc.vector.tensor_tensor(
-                out=by_cos[i][:, nh * NH:(nh + 1) * NH].rearrange("p (h d) -> p h d", d=HEAD),
-                in0=item_banks[i][nh][:].rearrange("p (h d) -> p h d", d=HEAD),
+                out=by_cos[key][:].rearrange("p (h d) -> p h d", d=HEAD),
+                in0=banks[key][:].rearrange("p (h d) -> p h d", d=HEAD),
                 in1=cos_tab[:, TABLE_OF_TILE[m], :].unsqueeze(1).to_broadcast([P, heads, HEAD]),
                 op=ALU.mult,
             )
             nc.vector.tensor_tensor(
-                out=by_sin[i][:, nh * NH:(nh + 1) * NH].rearrange("p (h u f) -> p h u f", u=2, f=HALF),
-                in0=item_banks[i][nh][:].rearrange("p (h u f) -> p h u f", u=2, f=HALF)[:, :, ::-1, :],
+                out=by_sin[key][:].rearrange("p (h u f) -> p h u f", u=2, f=HALF),
+                in0=banks[key][:].rearrange("p (h u f) -> p h u f", u=2, f=HALF)[:, :, ::-1, :],
                 in1=sin_tab[:, TABLE_OF_TILE[m], :].rearrange("p (u f) -> p u f", u=2).unsqueeze(1).to_broadcast([P, heads, 2, HALF]),
                 op=ALU.mult,
             )
 
-        def add_half(engine, i, nh):
+        def add(engine, w, m, nh, dst):
+            engine.tensor_tensor(out=dst, in0=by_cos[(w, m, nh)][:], in1=by_sin[(w, m, nh)][:], op=ALU.add)
+
+        def rotate_q_half(m, nh):
+            products(WQ, m, nh)
             if nh == 0:
-                rotated[i] = work.tile([P, D], F32, name="rotated", tag="rotated")
-            cols = slice(nh * NH, (nh + 1) * NH)
-            engine.tensor_tensor(out=rotated[i][:, cols], in0=by_cos[i][:, cols], in1=by_sin[i][:, cols], op=ALU.add)
+                rotated_q[m] = work.tile([P, D], F32, name="rotated_q", tag="rotated_q")
+            add(nc.gpsimd, WQ, m, nh, rotated_q[m][:, nh * NH:(nh + 1) * NH])
 
-        def store_item(i):
-            w, m = items[i]
-            store(w, m, rotated[i][:], slice(0, D))
+        def rotate_q(m):
+            rotate_q_half(m, 0)
+            rotate_q_half(m, 1)
+            store(WQ, m, rotated_q[m][:], slice(0, D))
 
-        def rotate(i):
-            for nh in range(2):
-                products(i, nh)
-                add_half(nc.gpsimd, i, nh)
-            store_item(i)
+        def finish_k(engine, m, nh):
+            rotated_k = work.tile([P, NH], F32, name="rotated_k", tag="rotated_k", bufs=PRODUCT_BUFS)
+            add(engine, WK, m, nh, rotated_k[:])
+            store(WK, m, rotated_k[:], slice(nh * NH, (nh + 1) * NH))
 
         v_banks = {}
 
-        def matmuls_v(nh):
-            for m in TILE_ORDER:
+        def matmuls_v(nh, tiles):
+            for m in tiles:
                 v_banks[(nh, m)] = multiply(v_psum, WV, m, nh)
 
         def copy_out_v(nh):
@@ -267,36 +269,46 @@ def tile_titanstnt_pa_kernel(tc, x, pmem, cos, sin, wq, wk, wv_bytes, wv_scale, 
                 nc.scalar.copy(out=v_both[:, b, :], in_=v_banks[(nh, 1 + b)][:])
             nc.sync.dma_start(out=outs[WV][:, P:2 * P, cols].rearrange("b p c -> p b c"), in_=v_both[:])
 
-        matmuls(0)
-        matmuls(1)
-        rotate(0)
-        matmuls(2)
-        rotate(1)
-        matmuls(3)
-        rotate(2)
-        quantize_pair(WK, 0)
-        products(3, 0)
-        add_half(nc.gpsimd, 3, 0)
-        quantize_pair(WK, 1)
-        matmuls(4)
-        products(3, 1)
-        add_half(nc.gpsimd, 3, 1)
-        store_item(3)
-        quantize_pair(WV, 0)
-        matmuls_v(0)
-        matmuls(5)
-        copy_out_v(0)
-        rotate(4)
-        matmuls(6)
-        quantize_pair(WV, 1)
-        matmuls_v(1)
-        copy_out_v(1)
-        rotate(5)
-        matmuls(7)
-        rotate(6)
-        products(7, 0)
-        products(7, 1)
+        t0, t1, t2, t3 = TILE_ORDER
+        for m in (t0, t1):
+            for nh in range(2):
+                matmuls(WQ, m, nh)
+        matmuls_v(0, (3, 0))
+        rotate_q(t0)
         for nh in range(2):
-            add_half(nc.vector, 7, nh)
-            cols = slice(nh * NH, (nh + 1) * NH)
-            store(items[7][0], items[7][1], rotated[7][:, cols], cols)
+            matmuls(WQ, t2, nh)
+        matmuls_v(0, (1, 2))
+        rotate_q(t1)
+        for nh in range(2):
+            matmuls(WQ, t3, nh)
+        quantize_pair(WV, 1)
+        rotate_q(t2)
+        rotate_q_half(t3, 0)
+        quantize_pair(WK, 0)
+        for m in (t0, t1, t2):
+            matmuls(WK, m, 0)
+        products(WQ, t3, 1)
+        copy_out_v(0)
+        add(nc.gpsimd, WQ, t3, 1, rotated_q[t3][:, NH:D])
+        store(WQ, t3, rotated_q[t3][:], slice(0, D))
+        matmuls(WK, t3, 0)
+        matmuls_v(1, TILE_ORDER)
+        for g in range(2):
+            interleave(nc.scalar.copy, WK, g, 1)
+        for m in (t0, t1, t2):
+            products(WK, m, 0)
+            finish_k(nc.gpsimd, m, 0)
+        products(WK, t3, 0)
+        quantize_pair(WK, 1)
+        for m in (t0, t1, t2):
+            matmuls(WK, m, 1)
+        finish_k(nc.vector, t3, 0)
+        matmuls(WK, t3, 1)
+        copy_out_v(1)
+        for m in (t0, t1):
+            products(WK, m, 1)
+            finish_k(nc.gpsimd, m, 1)
+        products(WK, t2, 1)
+        products(WK, t3, 1)
+        finish_k(nc.vector, t2, 1)
+        finish_k(nc.vector, t3, 1)

@@ -295,16 +295,19 @@ def tile_titanstnt_pa_kernel(tc, x, pmem, cos, sin, wq, wk, wv_bytes, wv_scale, 
         matmuls_v(1, TILE_ORDER)
         for g in range(2):
             interleave(nc.scalar.copy, WK, g, 1)
-        for m in (t0, t1, t2):
+        for m in (t0, t1):
             products(WK, m, 0)
             finish_k(nc.gpsimd, m, 0)
-        products(WK, t3, 0)
-        quantize_pair(WK, 1)
-        for m in (t0, t1, t2):
-            matmuls(WK, m, 1)
-        finish_k(nc.vector, t3, 0)
-        matmuls(WK, t3, 1)
         copy_out_v(1)
+        products(WK, t2, 0)
+        quantize_pair(WK, 1)
+        for m in (t0, t1):
+            matmuls(WK, m, 1)
+        finish_k(nc.gpsimd, t2, 0)
+        matmuls(WK, t2, 1)
+        products(WK, t3, 0)
+        finish_k(nc.gpsimd, t3, 0)
+        matmuls(WK, t3, 1)
         for m in (t0, t1):
             products(WK, m, 1)
             finish_k(nc.gpsimd, m, 1)

@@ -142,9 +142,10 @@ def tile_titanstnt_pa_kernel(tc, x, pmem, cos, sin, wq, wk, wv_bytes, wv_scale, 
                     out=wv_rows[g][:, j, :], in0=wv_codes_in[g][:, j, :].bitcast(FP8), scalar1=wv_scales[:, g, j:j + 1], scalar2=None, op0=ALU.mult
                 )
 
-        for g in range(2):
-            widen_on_vector(g, (0, 1))
-            widen_on_scalar(g, (2, 3))
+        widen_on_vector(0, (0, 1, 2))
+        widen_on_scalar(0, (3,))
+        widen_on_vector(1, (0, 1))
+        widen_on_scalar(1, (2, 3))
         interleave(nc.vector.tensor_copy, WQ, 0, 0)
         interleave(nc.vector.tensor_copy, WQ, 1, 0)
         interleave(nc.vector.tensor_copy, WQ, 0, 1)
@@ -166,15 +167,18 @@ def tile_titanstnt_pa_kernel(tc, x, pmem, cos, sin, wq, wk, wv_bytes, wv_scale, 
                         )
                 dst = x_grouped[:, g, 2 * P * tile_pair:2 * P * (tile_pair + 1), :].rearrange("p r t -> p (r t)").bitcast(F32)
                 nc.scalar.copy(out=dst.rearrange("p (i r u) -> p i r u", i=2, u=2), in_=turned[:].rearrange("p i u r -> p i r u"))
-        interleave(nc.vector.tensor_copy, WQ, 1, 1)
-        for g in range(2):
+        def quantize_x(g):
             nc.vector.quantize_mx(
                 out=x_codes[:, g, :].bitcast(FP8X4),
                 scales=x_scales[:, g, :],
                 in_=x_grouped[:, g, :, :].rearrange("p r t -> p (r t)"),
             )
-        quantize_unit(WQ, 1, 1)
+
         quantize_pair(WV, 0)
+        quantize_x(0)
+        interleave(nc.vector.tensor_copy, WQ, 1, 1)
+        quantize_x(1)
+        quantize_unit(WQ, 1, 1)
         nc.scalar.activation(out=sin_tab[:, :, 0:HALF], in_=sin_tab[:, :, 0:HALF], func=ACT.Copy, scale=-1.0)
         for g in range(2):
             interleave(nc.scalar.copy, WV, g, 1)

@@ -25,7 +25,7 @@ RUN = 8
 WQ, WK, WV = 0, 1, 2
 
 TABLE_OF_TILE = (0, 1, 1, 2)
-TILE_ORDER = (3, 0, 1, 2)
+TILE_ORDER = (0, 3, 1, 2)
 
 ITEM_BANKS = 4
 V_BANKS = 4
@@ -286,13 +286,13 @@ def tile_titanstnt_pa_kernel(tc, x, pmem, cos, sin, wq, wk, wv_bytes, wv_scale, 
         for nh in range(2):
             matmuls(WQ, t3, nh)
         quantize_pair(WV, 1)
+        copy_out_v(0)
         rotate_q(t2)
         rotate_q_half(t3, 0)
         quantize_pair(WK, 0)
         for m in (t0, t1, t2):
             matmuls(WK, m, 0)
         products(WQ, t3, 1)
-        copy_out_v(0)
         add(nc.gpsimd, WQ, t3, 1, rotated_q[t3][:, NH:D])
         store(WQ, t3, rotated_q[t3][:], slice(0, D))
         matmuls(WK, t3, 0)
@@ -307,10 +307,12 @@ def tile_titanstnt_pa_kernel(tc, x, pmem, cos, sin, wq, wk, wv_bytes, wv_scale, 
         quantize_pair(WK, 1)
         for m in (t0, t1):
             matmuls(WK, m, 1)
-        finish_k(nc.gpsimd, t2, 0)
+        k_both = work.tile([P, 2, NH], F32, name="k_both", tag="k_both", bufs=1)
+        add(nc.gpsimd, WK, t2, 0, k_both[:, t2 - 1, :])
         matmuls(WK, t2, 1)
         products(WK, t3, 0)
-        finish_k(nc.gpsimd, t3, 0)
+        add(nc.gpsimd, WK, t3, 0, k_both[:, t3 - 1, :])
+        nc.sync.dma_start(out=outs[WK][:, P:2 * P, 0:NH].rearrange("b p c -> p b c"), in_=k_both[:])
         matmuls(WK, t3, 1)
         for m in (t0, t1):
             products(WK, m, 1)

@@ -45,6 +45,8 @@ def tile_titanstnt_pa_kernel(tc, x, pmem, cos, sin, wq, wk, wv_bytes, wv_scale, 
 
         outs = [o.rearrange("b t h d -> b t (h d)") for o in (out_0, out_1, out_2)]
 
+        wv_scales = keep.tile([P, 2, PACK], F32, name="wv_scales", tag="wv_scales")
+        nc.scalar.dma_start(out=wv_scales[:], in_=wv_scale.rearrange("(g p j) o -> p g (j o)", p=P, j=PACK))
         warm_in = keep.tile([P, 8], F32, name="warm_in", tag="warm_in")
         warm_out = keep.tile([P, 8], F32, name="warm_out", tag="warm_out")
         nc.vector.memset(warm_in[:], 0.0)
@@ -62,8 +64,6 @@ def tile_titanstnt_pa_kernel(tc, x, pmem, cos, sin, wq, wk, wv_bytes, wv_scale, 
             nc.sync.dma_start(out=t[:], in_=wq_view[g][:, :, nh * NH:(nh + 1) * NH])
             rows[(WQ, g, nh)] = t[:]
 
-        wv_scales = keep.tile([P, 2, PACK], F32, name="wv_scales", tag="wv_scales")
-        nc.sync.dma_start(out=wv_scales[:], in_=wv_scale.rearrange("(g p j) o -> p g (j o)", p=P, j=PACK))
         wv_codes_in = [keep.tile([P, PACK, D], U8, name="wv_codes_in%d" % g, tag="wv_codes_in%d" % g) for g in range(2)]
         nc.sync.dma_start(out=wv_codes_in[0][:], in_=wv_view[0])
         nc.sync.dma_start(out=wv_codes_in[1][:], in_=wv_view[1])
@@ -320,4 +320,8 @@ def tile_titanstnt_pa_kernel(tc, x, pmem, cos, sin, wq, wk, wv_bytes, wv_scale, 
         products(WK, t2, 1)
         products(WK, t3, 1)
         finish_k(nc.vector, t2, 1)
-        finish_k(nc.vector, t3, 1)
+        last = work.tile([P, NH], F32, name="rotated_k", tag="rotated_k", bufs=PRODUCT_BUFS)
+        for h in range(NH // HEAD):
+            part = slice(h * HEAD, (h + 1) * HEAD)
+            nc.vector.tensor_tensor(out=last[:, part], in0=by_cos[(WK, t3, 1)][:, part], in1=by_sin[(WK, t3, 1)][:, part], op=ALU.add)
+            store(WK, t3, last[:, part], slice(NH + h * HEAD, NH + (h + 1) * HEAD))

@@ -287,16 +287,16 @@ def tile_titanstnt_pa_kernel(tc, x, pmem, cos, sin, wq, wk, wv_bytes, wv_scale, 
             matmuls(WQ, t3, nh)
         quantize_pair(WV, 1)
         copy_out_v(0)
+        matmuls_v(1, TILE_ORDER)
         rotate_q(t2)
-        rotate_q_half(t3, 0)
         quantize_pair(WK, 0)
-        for m in (t0, t1, t2):
+        for m in (t0, t1):
             matmuls(WK, m, 0)
-        products(WQ, t3, 1)
-        add(nc.gpsimd, WQ, t3, 1, rotated_q[t3][:, NH:D])
+        rotate_q_half(t3, 0)
+        matmuls(WK, t2, 0)
+        rotate_q_half(t3, 1)
         store(WQ, t3, rotated_q[t3][:], slice(0, D))
         matmuls(WK, t3, 0)
-        matmuls_v(1, TILE_ORDER)
         for g in range(2):
             interleave(nc.scalar.copy, WK, g, 1)
         for m in (t0, t1):

from contextlib import ExitStack

import concourse.mybir as mybir
from concourse.masks import make_identity

FLOPS = 2 * 640 * 1024 * 3072

F32 = mybir.dt.float32
BF16 = mybir.dt.bfloat16
U32 = mybir.dt.uint32
U8 = mybir.dt.uint8
FP8 = mybir.dt.float8_e4m3fn
FP8X4 = mybir.dt.float8_e4m3fn_x4
ALU = mybir.AluOpType
ACT = mybir.ActivationFunctionType

P = 128
PACK = 4
D = 1024
NH = 512
HEAD = 256
HALF = 128
X_REST = 64
RUN = 8
WQ, WK, WV = 0, 1, 2

TABLE_OF_TILE = (0, 1, 1, 2)
TILE_ORDER = (0, 3, 1, 2)

ITEM_BANKS = 4
V_BANKS = 4
ROT_BUFS = 4
PRODUCT_BUFS = 8
V_OUT_BUFS = 4


def tile_titanstnt_pa_kernel(tc, x, pmem, cos, sin, wq, wk, wv_bytes, wv_scale, out_0, out_1, out_2):
    nc = tc.nc
    with ExitStack() as ctx:
        keep = ctx.enter_context(tc.tile_pool(name="keep", bufs=1))
        work = ctx.enter_context(tc.tile_pool(name="work", bufs=ROT_BUFS))
        item_psum = ctx.enter_context(tc.psum_pool(name="item_psum", bufs=ITEM_BANKS))
        v_psum = ctx.enter_context(tc.psum_pool(name="v_psum", bufs=V_BANKS))
        ctx.enter_context(tc.manual_schedule())

        outs = [o.rearrange("b t h d -> b t (h d)") for o in (out_0, out_1, out_2)]

        wv_scales = keep.tile([P, 2, PACK], F32, name="wv_scales", tag="wv_scales")
        nc.scalar.dma_start(out=wv_scales[:], in_=wv_scale.rearrange("(g p j) o -> p g (j o)", p=P, j=PACK))
        warm_in = keep.tile([P, 8], F32, name="warm_in", tag="warm_in")
        warm_out = keep.tile([P, 8], F32, name="warm_out", tag="warm_out")
        nc.vector.memset(warm_in[:], 0.0)
        nc.scalar.activation(out=warm_out[:], in_=warm_in[:], func=ACT.Copy)
        ident = keep.tile([P, P], F32, name="ident", tag="ident")
        make_identity(nc, ident[:])

        wq_view = wq.rearrange("(g p j) n -> g p j n", p=P, j=PACK)
        wk_view = wk.rearrange("(g p j) n -> g p j n", p=P, j=PACK)
        wv_view = wv_bytes.rearrange("(g p j) n -> g p j n", p=P, j=PACK)
        rows = {}

        def load_wq_unit(g, nh):
            t = keep.tile([P, PACK, NH], BF16, name="wq_rows%d%d" % (g, nh), tag="wq_rows%d%d" % (g, nh))
            nc.sync.dma_start(out=t[:], in_=wq_view[g][:, :, nh * NH:(nh + 1) * NH])
            rows[(WQ, g, nh)] = t[:]

        wv_codes_in = [keep.tile([P, PACK, D], U8, name="wv_codes_in%d" % g, tag="wv_codes_in%d" % g) for g in range(2)]
        nc.sync.dma_start(out=wv_codes_in[0][:], in_=wv_view[0])
        nc.sync.dma_start(out=wv_codes_in[1][:], in_=wv_view[1])
        load_wq_unit(0, 0)
        load_wq_unit(1, 0)
        load_wq_unit(0, 1)
        x_pmem = keep.tile([P, D], BF16, name="x_pmem", tag="x_pmem")
        nc.sync.dma_start(out=x_pmem[:], in_=pmem[0])
        x_first = keep.tile([P, 2, D], BF16, name="x_first", tag="x_first")
        nc.sync.dma_start(out=x_first[:], in_=x[:, 0:P, :].rearrange("b p k -> p b k"))
        x_rest = keep.tile([P, D], BF16, name="x_rest", tag="x_rest")
        for b in range(2):
            nc.sync.dma_start(out=x_rest[b:P:2, :], in_=x[b, P:P + X_REST, :])
        load_wq_unit(1, 1)
        cos_tab = keep.tile([P, 3, HEAD], BF16, name="cos_tab", tag="cos_tab")
        sin_tab = keep.tile([P, 3, HEAD], BF16, name="sin_tab", tag="sin_tab")
        for tab, src in ((cos_tab, cos), (sin_tab, sin)):
            nc.sync.dma_start(out=tab[:, 0:2, :], in_=src[0:2 * P, :].rearrange("(a p) d -> p a d", p=P))
            for b in range(2):
                nc.sync.dma_start(out=tab[b:P:2, 2, :], in_=src[2 * P:2 * P + X_REST, :])
        for g in range(2):
            t = keep.tile([P, PACK, D], BF16, name="wk_rows%d" % g, tag="wk_rows%d" % g)
            nc.sync.dma_start(out=t[:], in_=wk_view[g])
            for nh in range(2):
                rows[(WK, g, nh)] = t[:, :, nh * NH:(nh + 1) * NH]

        w_codes = [keep.tile([P, 4, NH], U32, name="w_codes%d" % w, tag="w_codes%d" % w, align_bytes=64) for w in range(3)]
        w_scales = [keep.tile([P, 4, NH], U8, name="w_scales%d" % w, tag="w_scales%d" % w, align_bytes=64) for w in range(3)]
        x_grouped = keep.tile([P, 2, 4 * P, PACK], BF16, name="x_grouped", tag="x_grouped", align_bytes=64)
        x_codes = keep.tile([P, 2, 4 * P], U32, name="x_codes", tag="x_codes", align_bytes=64)
        x_scales = keep.tile([P, 2, 4 * P], U8, name="x_scales", tag="x_scales", align_bytes=64)
        grouped = {}

        def place(w, g, nh):
            return 2 * nh + g

        def interleave(copy, w, g, nh):
            at = place(w, g, nh)
            if (w, at // 2) not in grouped:
                tag = "grouped%d%d" % (w // 2, at // 2)
                grouped[(w, at // 2)] = keep.tile([P, 2, NH, PACK], BF16, name=tag, tag=tag, align_bytes=64)
            copy(
                out=grouped[(w, at // 2)][:, at % 2, :, :].rearrange("p (c i) j -> p c j i", i=RUN),
                in_=rows[(w, g, nh)].rearrange("p j (c i) -> p c j i", i=RUN),
            )

        def quantize_unit(w, g, nh):
            at = place(w, g, nh)
            nc.vector.quantize_mx(
                out=w_codes[w][:, at, :].bitcast(FP8X4),
                scales=w_scales[w][:, at, :],
                in_=grouped[(w, at // 2)][:, at % 2, :, :].rearrange("p c j -> p (c j)"),
            )

        def quantize_pair(w, pair):
            nc.vector.quantize_mx(
                out=w_codes[w][:, 2 * pair:2 * pair + 2, :].rearrange("p s c -> p (s c)").bitcast(FP8X4),
                scales=w_scales[w][:, 2 * pair:2 * pair + 2, :].rearrange("p s c -> p (s c)"),
                in_=grouped[(w, pair)][:].rearrange("p s c j -> p (s c j)"),
            )

        wv_rows = [keep.tile([P, PACK, D], BF16, name="wv_rows%d" % g, tag="wv_rows%d" % g) for g in range(2)]
        for g in range(2):
            for nh in range(2):
                rows[(WV, g, nh)] = wv_rows[g][:, :, nh * NH:(nh + 1) * NH]

        def widen_on_scalar(g, slots):
            for j in slots:
                nc.scalar.activation(
                    out=wv_rows[g][:, j, :], in_=wv_codes_in[g][:, j, :].bitcast(FP8), func=ACT.Copy, scale=wv_scales[:, g, j:j + 1]
                )

        def widen_on_vector(g, slots):
            for j in slots:
                nc.vector.tensor_scalar(
                    out=wv_rows[g][:, j, :], in0=wv_codes_in[g][:, j, :].bitcast(FP8), scalar1=wv_scales[:, g, j:j + 1], scalar2=None, op0=ALU.mult
                )

        widen_on_vector(0, (0, 1, 2))
        widen_on_scalar(0, (3,))
        widen_on_vector(1, (0, 1))
        widen_on_scalar(1, (2, 3))
        interleave(nc.vector.tensor_copy, WQ, 0, 0)
        interleave(nc.vector.tensor_copy, WQ, 1, 0)
        interleave(nc.vector.tensor_copy, WQ, 0, 1)
        quantize_unit(WQ, 0, 0)
        quantize_unit(WQ, 1, 0)
        quantize_unit(WQ, 0, 1)
        interleave(nc.scalar.copy, WV, 0, 0)
        interleave(nc.scalar.copy, WV, 1, 0)

        x_words = [x_pmem[:].bitcast(F32), x_first[:, 0, :].bitcast(F32), x_first[:, 1, :].bitcast(F32), x_rest[:].bitcast(F32)]
        words_of_pass = NH // 2
        for g in range(2):
            for tile_pair in range(2):
                turned = item_psum.tile([P, 2, 2, P], F32, name="turned", tag="bank")
                for i in range(2):
                    for u in range(2):
                        nc.tensor.transpose(
                            turned[:, i, u, :], x_words[2 * tile_pair + i][:, words_of_pass * g + u:words_of_pass * (g + 1):2], ident[:]
                        )
                dst = x_grouped[:, g, 2 * P * tile_pair:2 * P * (tile_pair + 1), :].rearrange("p r t -> p (r t)").bitcast(F32)
                nc.scalar.copy(out=dst.rearrange("p (i r u) -> p i r u", i=2, u=2), in_=turned[:].rearrange("p i u r -> p i r u"))
        def quantize_x(g):
            nc.vector.quantize_mx(
                out=x_codes[:, g, :].bitcast(FP8X4),
                scales=x_scales[:, g, :],
                in_=x_grouped[:, g, :, :].rearrange("p r t -> p (r t)"),
            )

        quantize_pair(WV, 0)
        quantize_x(0)
        interleave(nc.vector.tensor_copy, WQ, 1, 1)
        quantize_x(1)
        quantize_unit(WQ, 1, 1)
        nc.scalar.activation(out=sin_tab[:, :, 0:HALF], in_=sin_tab[:, :, 0:HALF], func=ACT.Copy, scale=-1.0)
        for g in range(2):
            interleave(nc.scalar.copy, WV, g, 1)
        for g in range(2):
            interleave(nc.scalar.copy, WK, g, 0)

        def multiply(pool, w, m, nh):
            bank = pool.tile([P, NH], F32, name="bank", tag="bank")
            for g in range(2):
                at = place(w, g, nh)
                nc.tensor.matmul_mx(
                    out=bank[:],
                    lhsT=x_codes[:, g, m * P:(m + 1) * P].bitcast(FP8X4),
                    lhsT_scale=x_scales[:, g, m * P:(m + 1) * P],
                    rhs=w_codes[w][:, at, :].bitcast(FP8X4),
                    rhs_scale=w_scales[w][:, at, :],
                    start=(g == 0),
                    stop=(g == 1),
                )
            return bank

        def store(w, m, src, cols):
            out = outs[w]
            if m == 0:
                width = src.shape[1]
                nc.sync.dma_start(out=out[:, 0:P, cols].rearrange("b p c -> p b c"), in_=src.unsqueeze(1).to_broadcast([P, 2, width]))
            elif m < 3:
                nc.sync.dma_start(out=out[m - 1, P:2 * P, cols], in_=src)
            else:
                for b in range(2):
                    nc.sync.dma_start(out=out[b, 2 * P:2 * P + X_REST, cols], in_=src[b:P:2, :])

        banks = {}
        by_cos = {}
        by_sin = {}
        rotated_q = {}

        def matmuls(w, m, nh):
            banks[(w, m, nh)] = multiply(item_psum, w, m, nh)

        def products(w, m, nh):
            key = (w, m, nh)
            by_cos[key] = work.tile([P, NH], F32, name="by_cos", tag="by_cos", bufs=PRODUCT_BUFS)
            by_sin[key] = work.tile([P, NH], F32, name="by_sin", tag="by_sin", bufs=PRODUCT_BUFS)
            heads = NH // HEAD
            nc.vector.tensor_tensor(
                out=by_cos[key][:].rearrange("p (h d) -> p h d", d=HEAD),
                in0=banks[key][:].rearrange("p (h d) -> p h d", d=HEAD),
                in1=cos_tab[:, TABLE_OF_TILE[m], :].unsqueeze(1).to_broadcast([P, heads, HEAD]),
                op=ALU.mult,
            )
            nc.vector.tensor_tensor(
                out=by_sin[key][:].rearrange("p (h u f) -> p h u f", u=2, f=HALF),
                in0=banks[key][:].rearrange("p (h u f) -> p h u f", u=2, f=HALF)[:, :, ::-1, :],
                in1=sin_tab[:, TABLE_OF_TILE[m], :].rearrange("p (u f) -> p u f", u=2).unsqueeze(1).to_broadcast([P, heads, 2, HALF]),
                op=ALU.mult,
            )

        def add(engine, w, m, nh, dst):
            engine.tensor_tensor(out=dst, in0=by_cos[(w, m, nh)][:], in1=by_sin[(w, m, nh)][:], op=ALU.add)

        def rotate_q_half(m, nh):
            products(WQ, m, nh)
            if nh == 0:
                rotated_q[m] = work.tile([P, D], F32, name="rotated_q", tag="rotated_q")
            add(nc.gpsimd, WQ, m, nh, rotated_q[m][:, nh * NH:(nh + 1) * NH])

        def rotate_q(m):
            rotate_q_half(m, 0)
            rotate_q_half(m, 1)
            store(WQ, m, rotated_q[m][:], slice(0, D))

        def finish_k(engine, m, nh):
            rotated_k = work.tile([P, NH], F32, name="rotated_k", tag="rotated_k", bufs=PRODUCT_BUFS)
            add(engine, WK, m, nh, rotated_k[:])
            store(WK, m, rotated_k[:], slice(nh * NH, (nh + 1) * NH))

        v_banks = {}

        def matmuls_v(nh, tiles):
            for m in tiles:
                v_banks[(nh, m)] = multiply(v_psum, WV, m, nh)

        def copy_out_v(nh):
            cols = slice(nh * NH, (nh + 1) * NH)
            for m in (3, 0):
                v_out = work.tile([P, NH], F32, name="v_out", tag="v_out", bufs=V_OUT_BUFS)
                nc.scalar.copy(out=v_out[:], in_=v_banks[(nh, m)][:])
                store(WV, m, v_out[:], cols)
            v_both = work.tile([P, 2, NH], F32, name="v_both", tag="v_both", bufs=2)
            for b in range(2):
                nc.scalar.copy(out=v_both[:, b, :], in_=v_banks[(nh, 1 + b)][:])
            nc.sync.dma_start(out=outs[WV][:, P:2 * P, cols].rearrange("b p c -> p b c"), in_=v_both[:])

        t0, t1, t2, t3 = TILE_ORDER
        for m in (t0, t1):
            for nh in range(2):
                matmuls(WQ, m, nh)
        matmuls_v(0, (3, 0))
        rotate_q(t0)
        for nh in range(2):
            matmuls(WQ, t2, nh)
        matmuls_v(0, (1, 2))
        rotate_q(t1)
        for nh in range(2):
            matmuls(WQ, t3, nh)
        quantize_pair(WV, 1)
        copy_out_v(0)
        matmuls_v(1, TILE_ORDER)
        rotate_q(t2)
        quantize_pair(WK, 0)
        for m in (t0, t1):
            matmuls(WK, m, 0)
        rotate_q_half(t3, 0)
        matmuls(WK, t2, 0)
        rotate_q_half(t3, 1)
        store(WQ, t3, rotated_q[t3][:], slice(0, D))
        matmuls(WK, t3, 0)
        for g in range(2):
            interleave(nc.scalar.copy, WK, g, 1)
        for m in (t0, t1):
            products(WK, m, 0)
            finish_k(nc.gpsimd, m, 0)
        copy_out_v(1)
        products(WK, t2, 0)
        quantize_pair(WK, 1)
        for m in (t0, t1):
            matmuls(WK, m, 1)
        k_both = work.tile([P, 2, NH], F32, name="k_both", tag="k_both", bufs=1)
        add(nc.gpsimd, WK, t2, 0, k_both[:, t2 - 1, :])
        matmuls(WK, t2, 1)
        products(WK, t3, 0)
        add(nc.gpsimd, WK, t3, 0, k_both[:, t3 - 1, :])
        nc.sync.dma_start(out=outs[WK][:, P:2 * P, 0:NH].rearrange("b p c -> p b c"), in_=k_both[:])
        matmuls(WK, t3, 1)
        for m in (t0, t1):
            products(WK, m, 1)
            finish_k(nc.gpsimd, m, 1)
        products(WK, t2, 1)
        products(WK, t3, 1)
        finish_k(nc.vector, t2, 1)
        last = work.tile([P, NH], F32, name="rotated_k", tag="rotated_k", bufs=PRODUCT_BUFS)
        for h in range(NH // HEAD):
            part = slice(h * HEAD, (h + 1) * HEAD)
            nc.vector.tensor_tensor(out=last[:, part], in0=by_cos[(WK, t3, 1)][:, part], in1=by_sin[(WK, t3, 1)][:, part], op=ALU.add)
            store(WK, t3, last[:, part], slice(NH + h * HEAD, NH + (h + 1) * HEAD))
